import numpy as np
import ml_dtypes


def mxq(x, axis, fmt="e4m3"):
    dtype, down = {"e4m3": (ml_dtypes.float8_e4m3fn, 7), "e5m2": (ml_dtypes.float8_e5m2, 14)}[fmt]
    v = np.moveaxis(np.asarray(x, np.float32).astype(ml_dtypes.bfloat16).astype(np.float64), axis, -1)
    blocks = v.reshape(v.shape[:-1] + (-1, 32))
    amax = np.abs(blocks).max(-1, keepdims=True)
    byte = np.maximum(np.where(amax > 0, np.frexp(amax)[1] - 1 + 127, 0) - down, 1)
    scale = np.exp2(byte - 127.0)
    codes = (blocks / scale).astype(np.float32).astype(dtype).astype(np.float64)
    return np.moveaxis((codes * scale).reshape(v.shape), -1, axis)


WIDE = False


def mx_kscale(k):
    if not WIDE:
        return np.ones(k)
    levels = np.array([10, -10, 5, -5, 0])
    a = np.random.permutation(np.resize(levels, k // 512 * 4)).reshape(k // 512, 4)
    idx = np.arange(k)
    return np.exp2(a[idx // 512, idx % 128 // 32])


BF16 = ml_dtypes.bfloat16


def bf(x):
    return np.asarray(x, np.float32).astype(BF16)


def f64(x):
    return np.asarray(x).astype(np.float64)


BATCH, IN_F, OUT_F, RANK, N_ADAPTERS = 8192, 512, 512, 128, 8
SEG = BATCH // N_ADAPTERS
LORA_GAIN = 2.0


def setup_inputs():
    s = mx_kscale(IN_F)
    return {"x": bf(np.random.standard_normal((BATCH, IN_F)) * s),
            "h_lora": bf(np.random.standard_normal((N_ADAPTERS, SEG, RANK))),
            "lora_B": bf(np.random.standard_normal((N_ADAPTERS, RANK, OUT_F)) * 0.5 / np.sqrt(RANK)),
            "M": bf(np.random.standard_normal((IN_F, OUT_F)) / np.sqrt(IN_F) / s[:, None])}


def reference(x, h_lora, lora_B, M):
    y = (f64(h_lora) @ f64(lora_B)) * LORA_GAIN
    y = y.reshape(BATCH, OUT_F)
    return y + (mxq(f64(x), 1, "e4m3") @ mxq(f64(M), 0, "e4m3"))

@@ -1,0 +1,211 @@
+from contextlib import ExitStack
+
+import concourse.mybir as mybir
+from concourse.masks import make_identity
+
+F32 = mybir.dt.float32
+BF16 = mybir.dt.bfloat16
+U32 = mybir.dt.uint32
+U8 = mybir.dt.uint8
+FP8X4 = mybir.dt.float8_e4m3fn_x4
+ADD = mybir.AluOpType.add
+
+P = 128
+ROWS, IN_F, OUT_F, RANK, SEGS = 8192, 512, 512, 128, 8
+SEG_ROWS = ROWS // SEGS
+TILES = SEG_ROWS // P
+WORDS = IN_F // 2
+PAIRS = SEGS * TILES // 2
+QUAD = 4
+GAIN = 2.0
+
+FLOPS = 2 * ROWS * IN_F * OUT_F + 2 * ROWS * RANK * OUT_F
+
+STAGE_BUFS = 10
+LO_BANKS = 3
+MX_BANKS = 2
+
+
+def tile_lorasequential_pa_t_kernel(tc, x, h_lora, lora_B, M, out):
+    nc = tc.nc
+    with ExitStack() as ctx:
+        ctx.enter_context(tc.manual_schedule())
+        keep = ctx.enter_context(tc.tile_pool(name="keep", bufs=1))
+        grp_pool = ctx.enter_context(tc.tile_pool(name="grp", bufs=3))
+        ht_pool = ctx.enter_context(tc.tile_pool(name="ht", bufs=2))
+        stage = ctx.enter_context(tc.tile_pool(name="stage", bufs=STAGE_BUFS))
+        ps_x = ctx.enter_context(tc.psum_pool(name="psx", bufs=2))
+        ps_h = ctx.enter_context(tc.psum_pool(name="psh", bufs=1))
+        ps_l = ctx.enter_context(tc.psum_pool(name="psl", bufs=LO_BANKS))
+        ps_m = ctx.enter_context(tc.psum_pool(name="psm", bufs=MX_BANKS))
+
+        x_v = x.rearrange("(g p t) k -> g p (t k)", p=P, t=TILES)
+        h_v = h_lora.rearrange("g (p t) r -> p g (t r)", t=TILES)
+        b_v = lora_B.rearrange("g r n -> r g n")
+        m_v = M.rearrange("(u q e) c -> q u (e c)", u=2, e=2)
+        o_v = out.rearrange("(g p t) n -> g p t n", p=P, t=TILES)
+
+        warm_in = keep.tile([P, 1], F32)
+        warm_out = keep.tile([P, 1], F32)
+        nc.vector.memset(warm_in[:], 0.0)
+        nc.scalar.mul(out=warm_out[:], in_=warm_in[:], mul=GAIN)
+
+        ident_f = keep.tile([P, P], F32)
+        make_identity(nc, ident_f[:])
+        ident_b = keep.tile([P, P], BF16)
+        make_identity(nc, ident_b[:])
+
+        m_raw = keep.tile([P, 4, OUT_F], BF16)
+        x_sb = [keep.tile([P, TILES * IN_F], BF16, name="x%d" % g) for g in range(SEGS)]
+        h_sb = keep.tile([P, SEGS, TILES * RANK], BF16)
+        b_sb = keep.tile([P, SEGS, OUT_F], BF16)
+
+        def load_x(g, t0, t1):
+            nc.sync.dma_start(out=x_sb[g][:, t0 * IN_F : t1 * IN_F], in_=x_v[g][:, t0 * IN_F : t1 * IN_F])
+
+        def load_hb(g0, g1):
+            nc.sync.dma_start(out=h_sb[:, g0:g1, :], in_=h_v[:, g0:g1, :])
+            nc.sync.dma_start(out=b_sb[:, g0:g1, :], in_=b_v[:, g0:g1, :])
+
+        nc.sync.dma_start(out=m_raw[:].rearrange("p (u e) c -> p u (e c)", u=2), in_=m_v)
+        load_x(0, 0, 2)
+        load_hb(0, 1)
+        load_x(0, 2, 4)
+        load_x(0, 4, 8)
+        load_x(1, 0, 4)
+        load_hb(1, 2)
+        load_x(1, 4, 8)
+        load_x(2, 0, 8)
+        load_hb(2, 4)
+        load_x(3, 0, 8)
+        load_x(4, 0, 8)
+        load_hb(4, 8)
+        load_x(5, 0, 8)
+        load_x(6, 0, 8)
+        load_x(7, 0, 8)
+
+        m_grp = keep.tile([P, OUT_F, 4], BF16, align_bytes=64)
+        m_codes = keep.tile([P, OUT_F], U32, align_bytes=64)
+        m_scales = keep.tile([P, OUT_F], U8, align_bytes=64)
+        nc.vector.tensor_copy(out=m_grp[:], in_=m_raw[:].rearrange("p t c -> p c t"))
+        nc.vector.quantize_mx(
+            out=m_codes[:].bitcast(FP8X4),
+            scales=m_scales[:],
+            in_=m_grp[:].rearrange("p c t -> p (c t)"),
+        )
+
+        xt_of = {}
+        grp_of = {}
+        q_of = {}
+        ht_of = {}
+        o_of = {}
+
+        def transpose_x(i):
+            xt = ps_x.tile([P, 2, 2 * P], F32)
+            for j in range(2):
+                g, t = divmod(2 * i + j, TILES)
+                words = x_sb[g][:].bitcast(F32)
+                for u in range(2):
+                    w0 = t * WORDS + u * P
+                    nc.tensor.transpose(xt[:, u, j * P : (j + 1) * P], words[:, w0 : w0 + P], ident_f[:])
+            xt_of[i] = xt
+
+        def copy_x(i):
+            grp = grp_pool.tile([P, 8 * P], BF16, align_bytes=64)
+            nc.scalar.copy(
+                out=grp[:].bitcast(F32).rearrange("p (c u) -> p c u", u=2),
+                in_=xt_of[i][:].rearrange("p u c -> p c u"),
+            )
+            grp_of[i] = grp
+
+        def quantise_x(i):
+            codes = grp_pool.tile([P, 2 * P], U32, align_bytes=64)
+            scales = grp_pool.tile([P, 2 * P], U8, align_bytes=64)
+            nc.vector.quantize_mx(out=codes[:].bitcast(FP8X4), scales=scales[:], in_=grp_of[i][:])
+            q_of[i] = (codes, scales)
+
+        def transpose_h(g):
+            hp = ps_h.tile([P, TILES, P], BF16)
+            for t in range(TILES):
+                nc.tensor.transpose(hp[:, t, :], h_sb[:, g, t * RANK : (t + 1) * RANK], ident_b[:])
+            return hp
+
+        def copy_h(g, hp):
+            ht = ht_pool.tile([P, TILES, P], BF16)
+            nc.vector.tensor_copy(out=ht[:], in_=hp[:])
+            ht_of[g] = ht
+
+        def lora(n):
+            g, t = divmod(n, TILES)
+            lo = ps_l.tile([P, OUT_F], F32)
+            nc.tensor.matmul(lo[:], lhsT=ht_of[g][:, t, :], rhs=b_sb[:, g, :], start=True, stop=True)
+            return lo
+
+        def base(n):
+            codes, scales = q_of[n // 2]
+            cols = slice((n % 2) * P, (n % 2 + 1) * P)
+            mx = ps_m.tile([P, OUT_F], F32)
+            nc.tensor.matmul_mx(
+                out=mx[:],
+                lhsT=codes[:, cols].bitcast(FP8X4),
+                lhsT_scale=scales[:, cols],
+                rhs=m_codes[:].bitcast(FP8X4),
+                rhs_scale=m_scales[:],
+                start=True,
+                stop=True,
+            )
+            return mx
+
+        def lora_out(n, lo):
+            if n % QUAD == 0:
+                o_sb = stage.tile([P, QUAD, OUT_F], F32)
+                o_of[n // QUAD] = o_sb
+            nc.scalar.mul(out=o_of[n // QUAD][:, n % QUAD, :], in_=lo[:], mul=GAIN)
+
+        def add_base(n, mx):
+            o_part = o_of[n // QUAD][:, n % QUAD, :]
+            nc.vector.tensor_tensor(out=o_part, in0=mx[:], in1=o_part, op=ADD)
+
+        def store(n0, n1):
+            g, t0 = divmod(n0, TILES)
+            nc.sync.dma_start(
+                out=o_v[g][:, t0 : t0 + n1 - n0, :],
+                in_=o_of[n0 // QUAD][:, n0 % QUAD : n0 % QUAD + n1 - n0, :],
+            )
+
+        transpose_x(0)
+        copy_x(0)
+        hp0 = transpose_h(0)
+        copy_h(0, hp0)
+        transpose_x(1)
+        copy_x(1)
+        quantise_x(0)
+
+        for i in range(PAIRS):
+            a, b = 2 * i, 2 * i + 1
+            g = a // TILES
+            next_h = i % 4 == 2 and g + 1 < SEGS
+            lo_a = lora(a)
+            if i + 2 < PAIRS:
+                transpose_x(i + 2)
+            if next_h:
+                hp = transpose_h(g + 1)
+            lo_b = lora(b)
+            mx_a = base(a)
+            mx_b = base(b)
+            lora_out(a, lo_a)
+            lora_out(b, lo_b)
+            if i + 2 < PAIRS:
+                copy_x(i + 2)
+            if i + 1 < PAIRS:
+                quantise_x(i + 1)
+            add_base(a, mx_a)
+            add_base(b, mx_b)
+            if next_h:
+                copy_h(g + 1, hp)
+            if i == PAIRS - 1:
+                store(a, b + 1)
+            elif i == PAIRS - 2:
+                store(a, b + 1)
+            elif i % 2 == 1:
+                store(a - 2, b + 1)

@@ -31,7 +31,7 @@ def tile_lorasequential_pa_t_kernel(tc, x, h_lora, lora_B, M, out):
     with ExitStack() as ctx:
         ctx.enter_context(tc.manual_schedule())
         keep = ctx.enter_context(tc.tile_pool(name="keep", bufs=1))
-        grp_pool = ctx.enter_context(tc.tile_pool(name="grp", bufs=3))
+        grp_pool = ctx.enter_context(tc.tile_pool(name="grp", bufs=4))
         ht_pool = ctx.enter_context(tc.tile_pool(name="ht", bufs=2))
         stage = ctx.enter_context(tc.tile_pool(name="stage", bufs=STAGE_BUFS))
         ps_x = ctx.enter_context(tc.psum_pool(name="psx", bufs=2))
@@ -174,38 +174,45 @@ def tile_lorasequential_pa_t_kernel(tc, x, h_lora, lora_B, M, out):
             )
 
         transpose_x(0)
-        copy_x(0)
         hp0 = transpose_h(0)
-        copy_h(0, hp0)
         transpose_x(1)
+        copy_x(0)
         copy_x(1)
+        copy_h(0, hp0)
         quantise_x(0)
+        quantise_x(1)
 
-        for i in range(PAIRS):
-            a, b = 2 * i, 2 * i + 1
-            g = a // TILES
-            next_h = i % 4 == 2 and g + 1 < SEGS
-            lo_a = lora(a)
-            if i + 2 < PAIRS:
-                transpose_x(i + 2)
+        for k in range(PAIRS // 2):
+            n = QUAD * k
+            g = n // TILES
+            more = 2 * k + 2 < PAIRS
+            next_h = k % 2 == 1 and g + 1 < SEGS
+            last = k == PAIRS // 2 - 1
+            if more:
+                transpose_x(2 * k + 2)
+                transpose_x(2 * k + 3)
             if next_h:
                 hp = transpose_h(g + 1)
-            lo_b = lora(b)
-            mx_a = base(a)
-            mx_b = base(b)
-            lora_out(a, lo_a)
-            lora_out(b, lo_b)
-            if i + 2 < PAIRS:
-                copy_x(i + 2)
-            if i + 1 < PAIRS:
-                quantise_x(i + 1)
-            add_base(a, mx_a)
-            add_base(b, mx_b)
+            los = [lora(n + j) for j in range(QUAD)]
+            mxs = [base(n + j) for j in range(QUAD)]
+            if more:
+                copy_x(2 * k + 2)
+                copy_x(2 * k + 3)
+            for j in range(QUAD):
+                lora_out(n + j, los[j])
             if next_h:
                 copy_h(g + 1, hp)
-            if i == PAIRS - 1:
-                store(a, b + 1)
-            elif i == PAIRS - 2:
-                store(a, b + 1)
-            elif i % 2 == 1:
-                store(a - 2, b + 1)
+            add_base(n, mxs[0])
+            add_base(n + 1, mxs[1])
+            if last:
+                store(n, n + 2)
+            if more:
+                quantise_x(2 * k + 2)
+            add_base(n + 2, mxs[2])
+            add_base(n + 3, mxs[3])
+            if last:
+                store(n + 2, n + 4)
+            else:
+                store(n, n + 4)
+            if more:
+                quantise_x(2 * k + 3)

@@ -9,6 +9,7 @@ U32 = mybir.dt.uint32
 U8 = mybir.dt.uint8
 FP8X4 = mybir.dt.float8_e4m3fn_x4
 ADD = mybir.AluOpType.add
+MULT = mybir.AluOpType.mult
 
 P = 128
 ROWS, IN_F, OUT_F, RANK, SEGS = 8192, 512, 512, 128, 8
@@ -22,8 +23,8 @@ GAIN = 2.0
 FLOPS = 2 * ROWS * IN_F * OUT_F + 2 * ROWS * RANK * OUT_F
 
 STAGE_BUFS = 10
-LO_BANKS = 3
-MX_BANKS = 2
+LO_BANKS = 2
+MX_BANKS = 3
 
 
 def tile_lorasequential_pa_t_kernel(tc, x, h_lora, lora_B, M, out):
@@ -31,7 +32,7 @@ def tile_lorasequential_pa_t_kernel(tc, x, h_lora, lora_B, M, out):
     with ExitStack() as ctx:
         ctx.enter_context(tc.manual_schedule())
         keep = ctx.enter_context(tc.tile_pool(name="keep", bufs=1))
-        grp_pool = ctx.enter_context(tc.tile_pool(name="grp", bufs=4))
+        grp_pool = ctx.enter_context(tc.tile_pool(name="grp", bufs=3))
         ht_pool = ctx.enter_context(tc.tile_pool(name="ht", bufs=2))
         stage = ctx.enter_context(tc.tile_pool(name="stage", bufs=STAGE_BUFS))
         ps_x = ctx.enter_context(tc.psum_pool(name="psx", bufs=2))
@@ -44,11 +45,6 @@ def tile_lorasequential_pa_t_kernel(tc, x, h_lora, lora_B, M, out):
         b_v = lora_B.rearrange("g r n -> r g n")
         m_v = M.rearrange("(u q e) c -> q u (e c)", u=2, e=2)
         o_v = out.rearrange("(g p t) n -> g p t n", p=P, t=TILES)
-
-        warm_in = keep.tile([P, 1], F32)
-        warm_out = keep.tile([P, 1], F32)
-        nc.vector.memset(warm_in[:], 0.0)
-        nc.scalar.mul(out=warm_out[:], in_=warm_in[:], mul=GAIN)
 
         ident_f = keep.tile([P, P], F32)
         make_identity(nc, ident_f[:])
@@ -160,11 +156,11 @@ def tile_lorasequential_pa_t_kernel(tc, x, h_lora, lora_B, M, out):
             if n % QUAD == 0:
                 o_sb = stage.tile([P, QUAD, OUT_F], F32)
                 o_of[n // QUAD] = o_sb
-            nc.scalar.mul(out=o_of[n // QUAD][:, n % QUAD, :], in_=lo[:], mul=GAIN)
+            nc.scalar.copy(out=o_of[n // QUAD][:, n % QUAD, :], in_=lo[:])
 
         def add_base(n, mx):
             o_part = o_of[n // QUAD][:, n % QUAD, :]
-            nc.vector.tensor_tensor(out=o_part, in0=mx[:], in1=o_part, op=ADD)
+            nc.vector.scalar_tensor_tensor(out=o_part, in0=o_part, scalar=GAIN, in1=mx[:], op0=MULT, op1=ADD)
 
         def store(n0, n1):
             g, t0 = divmod(n0, TILES)
@@ -174,45 +170,40 @@ def tile_lorasequential_pa_t_kernel(tc, x, h_lora, lora_B, M, out):
             )
 
         transpose_x(0)
-        hp0 = transpose_h(0)
-        transpose_x(1)
         copy_x(0)
-        copy_x(1)
+        hp0 = transpose_h(0)
         copy_h(0, hp0)
+        transpose_x(1)
+        copy_x(1)
         quantise_x(0)
-        quantise_x(1)
 
-        for k in range(PAIRS // 2):
-            n = QUAD * k
-            g = n // TILES
-            more = 2 * k + 2 < PAIRS
-            next_h = k % 2 == 1 and g + 1 < SEGS
-            last = k == PAIRS // 2 - 1
-            if more:
-                transpose_x(2 * k + 2)
-                transpose_x(2 * k + 3)
+        for i in range(PAIRS):
+            a, b = 2 * i, 2 * i + 1
+            g = a // TILES
+            next_h = i % 4 == 2 and g + 1 < SEGS
+            lo_a = lora(a)
+            if i + 2 < PAIRS:
+                transpose_x(i + 2)
             if next_h:
                 hp = transpose_h(g + 1)
-            los = [lora(n + j) for j in range(QUAD)]
-            mxs = [base(n + j) for j in range(QUAD)]
-            if more:
-                copy_x(2 * k + 2)
-                copy_x(2 * k + 3)
-            for j in range(QUAD):
-                lora_out(n + j, los[j])
+            lo_b = lora(b)
+            mx_a = base(a)
+            mx_b = base(b)
+            lora_out(a, lo_a)
+            lora_out(b, lo_b)
+            if i + 2 < PAIRS:
+                copy_x(i + 2)
+            if i + 1 < PAIRS:
+                quantise_x(i + 1)
+            add_base(a, mx_a)
+            if i == PAIRS - 1:
+                store(a, a + 1)
+            add_base(b, mx_b)
             if next_h:
                 copy_h(g + 1, hp)
-            add_base(n, mxs[0])
-            add_base(n + 1, mxs[1])
-            if last:
-                store(n, n + 2)
-            if more:
-                quantise_x(2 * k + 2)
-            add_base(n + 2, mxs[2])
-            add_base(n + 3, mxs[3])
-            if last:
-                store(n + 2, n + 4)
-            else:
-                store(n, n + 4)
-            if more:
-                quantise_x(2 * k + 3)
+            if i == PAIRS - 1:
+                store(b, b + 1)
+            elif i == PAIRS - 2:
+                store(a, b + 1)
+            elif i % 2 == 1:
+                store(a - 2, b + 1)

@@ -59,23 +59,29 @@ def tile_lorasequential_pa_t_kernel(tc, x, h_lora, lora_B, M, out):
         def load_x(g, t0, t1):
             nc.sync.dma_start(out=x_sb[g][:, t0 * IN_F : t1 * IN_F], in_=x_v[g][:, t0 * IN_F : t1 * IN_F])
 
-        def load_hb(g0, g1):
+        def load_h(g0, g1):
             nc.sync.dma_start(out=h_sb[:, g0:g1, :], in_=h_v[:, g0:g1, :])
+
+        def load_b(g0, g1):
             nc.sync.dma_start(out=b_sb[:, g0:g1, :], in_=b_v[:, g0:g1, :])
 
         nc.sync.dma_start(out=m_raw[:].rearrange("p (u e) c -> p u (e c)", u=2), in_=m_v)
         load_x(0, 0, 2)
-        load_hb(0, 1)
+        load_h(0, 1)
+        load_b(0, 1)
         load_x(0, 2, 4)
         load_x(0, 4, 8)
+        load_h(1, 2)
         load_x(1, 0, 4)
-        load_hb(1, 2)
+        load_b(1, 2)
         load_x(1, 4, 8)
         load_x(2, 0, 8)
-        load_hb(2, 4)
+        load_h(2, 4)
+        load_b(2, 4)
         load_x(3, 0, 8)
         load_x(4, 0, 8)
-        load_hb(4, 8)
+        load_h(4, 8)
+        load_b(4, 8)
         load_x(5, 0, 8)
         load_x(6, 0, 8)
         load_x(7, 0, 8)
@@ -120,11 +126,9 @@ def tile_lorasequential_pa_t_kernel(tc, x, h_lora, lora_B, M, out):
             nc.vector.quantize_mx(out=codes[:].bitcast(FP8X4), scales=scales[:], in_=grp_of[i][:])
             q_of[i] = (codes, scales)
 
-        def transpose_h(g):
-            hp = ps_h.tile([P, TILES, P], BF16)
-            for t in range(TILES):
+        def transpose_h(g, hp, t0, t1):
+            for t in range(t0, t1):
                 nc.tensor.transpose(hp[:, t, :], h_sb[:, g, t * RANK : (t + 1) * RANK], ident_b[:])
-            return hp
 
         def copy_h(g, hp):
             ht = ht_pool.tile([P, TILES, P], BF16)
@@ -171,26 +175,43 @@ def tile_lorasequential_pa_t_kernel(tc, x, h_lora, lora_B, M, out):
 
         transpose_x(0)
         copy_x(0)
-        hp0 = transpose_h(0)
-        copy_h(0, hp0)
+        hp = ps_h.tile([P, TILES, P], BF16)
+        transpose_h(0, hp, 0, TILES)
+        copy_h(0, hp)
         transpose_x(1)
         copy_x(1)
+        lo_of = {0: lora(0), 1: lora(1)}
+        lora_out(0, lo_of[0])
+        lora_out(1, lo_of[1])
         quantise_x(0)
 
         for i in range(PAIRS):
             a, b = 2 * i, 2 * i + 1
             g = a // TILES
-            next_h = i % 4 == 2 and g + 1 < SEGS
-            lo_a = lora(a)
+            s = i % 4
+            more_h = g + 1 < SEGS
+            more_l = i + 1 < PAIRS
+            early = i == 0
+            if early:
+                mx_a = base(a)
+                mx_b = base(b)
+            if more_l:
+                lo_of[a + 2] = lora(a + 2)
             if i + 2 < PAIRS:
                 transpose_x(i + 2)
-            if next_h:
-                hp = transpose_h(g + 1)
-            lo_b = lora(b)
-            mx_a = base(a)
-            mx_b = base(b)
-            lora_out(a, lo_a)
-            lora_out(b, lo_b)
+            if more_h and s == 0:
+                hp = ps_h.tile([P, TILES, P], BF16)
+                transpose_h(g + 1, hp, 0, TILES // 2)
+            if more_h and s == 1:
+                transpose_h(g + 1, hp, TILES // 2, TILES)
+            if more_l:
+                lo_of[b + 2] = lora(b + 2)
+            if not early:
+                mx_a = base(a)
+                mx_b = base(b)
+            if more_l:
+                lora_out(a + 2, lo_of[a + 2])
+                lora_out(b + 2, lo_of[b + 2])
             if i + 2 < PAIRS:
                 copy_x(i + 2)
             if i + 1 < PAIRS:
@@ -199,7 +220,7 @@ def tile_lorasequential_pa_t_kernel(tc, x, h_lora, lora_B, M, out):
             if i == PAIRS - 1:
                 store(a, a + 1)
             add_base(b, mx_b)
-            if next_h:
+            if more_h and s == 1:
                 copy_h(g + 1, hp)
             if i == PAIRS - 1:
                 store(b, b + 1)

@@ -18,6 +18,8 @@ TILES = SEG_ROWS // P
 WORDS = IN_F // 2
 PAIRS = SEGS * TILES // 2
 QUAD = 4
+HALF = TILES // 2
+M_SHARE = 128
 GAIN = 2.0
 
 FLOPS = 2 * ROWS * IN_F * OUT_F + 2 * ROWS * RANK * OUT_F
@@ -65,11 +67,12 @@ def tile_lorasequential_pa_t_kernel(tc, x, h_lora, lora_B, M, out):
         def load_b(g0, g1):
             nc.sync.dma_start(out=b_sb[:, g0:g1, :], in_=b_v[:, g0:g1, :])
 
-        nc.sync.dma_start(out=m_raw[:].rearrange("p (u e) c -> p u (e c)", u=2), in_=m_v)
         load_x(0, 0, 2)
-        load_h(0, 1)
+        nc.sync.dma_start(out=h_sb[:, 0, 0 : HALF * RANK], in_=h_v[:, 0, 0 : HALF * RANK])
         load_b(0, 1)
+        nc.sync.dma_start(out=m_raw[:].rearrange("p (u e) c -> p u (e c)", u=2), in_=m_v)
         load_x(0, 2, 4)
+        nc.sync.dma_start(out=h_sb[:, 0, HALF * RANK :], in_=h_v[:, 0, HALF * RANK :])
         load_x(0, 4, 8)
         load_h(1, 2)
         load_x(1, 0, 4)
@@ -89,12 +92,16 @@ def tile_lorasequential_pa_t_kernel(tc, x, h_lora, lora_B, M, out):
         m_grp = keep.tile([P, OUT_F, 4], BF16, align_bytes=64)
         m_codes = keep.tile([P, OUT_F], U32, align_bytes=64)
         m_scales = keep.tile([P, OUT_F], U8, align_bytes=64)
-        nc.vector.tensor_copy(out=m_grp[:], in_=m_raw[:].rearrange("p t c -> p c t"))
-        nc.vector.quantize_mx(
-            out=m_codes[:].bitcast(FP8X4),
-            scales=m_scales[:],
-            in_=m_grp[:].rearrange("p c t -> p (c t)"),
-        )
+
+        def interleave_m(copy, c0, c1):
+            copy(out=m_grp[:, c0:c1, :], in_=m_raw[:, :, c0:c1].rearrange("p t c -> p c t"))
+
+        def quantise_m():
+            nc.vector.quantize_mx(
+                out=m_codes[:].bitcast(FP8X4),
+                scales=m_scales[:],
+                in_=m_grp[:].rearrange("p c t -> p (c t)"),
+            )
 
         xt_of = {}
         grp_of = {}
@@ -130,10 +137,11 @@ def tile_lorasequential_pa_t_kernel(tc, x, h_lora, lora_B, M, out):
             for t in range(t0, t1):
                 nc.tensor.transpose(hp[:, t, :], h_sb[:, g, t * RANK : (t + 1) * RANK], ident_b[:])
 
-        def copy_h(g, hp):
-            ht = ht_pool.tile([P, TILES, P], BF16)
-            nc.vector.tensor_copy(out=ht[:], in_=hp[:])
-            ht_of[g] = ht
+        def copy_h(g, hp, t0, t1):
+            if t0 == 0:
+                ht = ht_pool.tile([P, TILES, P], BF16)
+                ht_of[g] = ht
+            nc.vector.tensor_copy(out=ht_of[g][:, t0:t1, :], in_=hp[:, t0:t1, :])
 
         def lora(n):
             g, t = divmod(n, TILES)
@@ -176,14 +184,19 @@ def tile_lorasequential_pa_t_kernel(tc, x, h_lora, lora_B, M, out):
         transpose_x(0)
         copy_x(0)
         hp = ps_h.tile([P, TILES, P], BF16)
-        transpose_h(0, hp, 0, TILES)
-        copy_h(0, hp)
-        transpose_x(1)
-        copy_x(1)
+        transpose_h(0, hp, 0, HALF)
+        copy_h(0, hp, 0, HALF)
+        quantise_x(0)
+        interleave_m(nc.scalar.copy, 0, M_SHARE)
+        interleave_m(nc.vector.tensor_copy, M_SHARE, OUT_F)
+        quantise_m()
         lo_of = {0: lora(0), 1: lora(1)}
         lora_out(0, lo_of[0])
         lora_out(1, lo_of[1])
-        quantise_x(0)
+        transpose_x(1)
+        copy_x(1)
+        transpose_h(0, hp, HALF, TILES)
+        copy_h(0, hp, HALF, TILES)
 
         for i in range(PAIRS):
             a, b = 2 * i, 2 * i + 1
@@ -221,10 +234,10 @@ def tile_lorasequential_pa_t_kernel(tc, x, h_lora, lora_B, M, out):
                 store(a, a + 1)
             add_base(b, mx_b)
             if more_h and s == 1:
-                copy_h(g + 1, hp)
+                copy_h(g + 1, hp, 0, TILES)
             if i == PAIRS - 1:
                 store(b, b + 1)
-            elif i == PAIRS - 2:
+            elif i >= PAIRS - 4:
                 store(a, b + 1)
             elif i % 2 == 1:
                 store(a - 2, b + 1)

@@ -17,14 +17,13 @@ SEG_ROWS = ROWS // SEGS
 TILES = SEG_ROWS // P
 WORDS = IN_F // 2
 PAIRS = SEGS * TILES // 2
-QUAD = 4
 HALF = TILES // 2
 M_SHARE = 128
 GAIN = 2.0
 
 FLOPS = 2 * ROWS * IN_F * OUT_F + 2 * ROWS * RANK * OUT_F
 
-STAGE_BUFS = 10
+STAGE_BUFS = 6
 LO_BANKS = 2
 MX_BANKS = 3
 
@@ -68,16 +67,13 @@ def tile_lorasequential_pa_t_kernel(tc, x, h_lora, lora_B, M, out):
             nc.sync.dma_start(out=b_sb[:, g0:g1, :], in_=b_v[:, g0:g1, :])
 
         load_x(0, 0, 2)
-        nc.sync.dma_start(out=h_sb[:, 0, 0 : HALF * RANK], in_=h_v[:, 0, 0 : HALF * RANK])
+        load_h(0, 1)
         load_b(0, 1)
         nc.sync.dma_start(out=m_raw[:].rearrange("p (u e) c -> p u (e c)", u=2), in_=m_v)
-        load_x(0, 2, 4)
-        nc.sync.dma_start(out=h_sb[:, 0, HALF * RANK :], in_=h_v[:, 0, HALF * RANK :])
-        load_x(0, 4, 8)
+        load_x(0, 2, 8)
         load_h(1, 2)
-        load_x(1, 0, 4)
         load_b(1, 2)
-        load_x(1, 4, 8)
+        load_x(1, 0, 8)
         load_x(2, 0, 8)
         load_h(2, 4)
         load_b(2, 4)
@@ -165,20 +161,22 @@ def tile_lorasequential_pa_t_kernel(tc, x, h_lora, lora_B, M, out):
             return mx
 
         def lora_out(n, lo):
-            if n % QUAD == 0:
-                o_sb = stage.tile([P, QUAD, OUT_F], F32)
-                o_of[n // QUAD] = o_sb
-            nc.scalar.copy(out=o_of[n // QUAD][:, n % QUAD, :], in_=lo[:])
+            g, t = divmod(n, TILES)
+            if t == 0:
+                o_sb = stage.tile([P, TILES, OUT_F], F32)
+                o_of[g] = o_sb
+            nc.scalar.copy(out=o_of[g][:, t, :], in_=lo[:])
 
         def add_base(n, mx):
-            o_part = o_of[n // QUAD][:, n % QUAD, :]
+            g, t = divmod(n, TILES)
+            o_part = o_of[g][:, t, :]
             nc.vector.scalar_tensor_tensor(out=o_part, in0=o_part, scalar=GAIN, in1=mx[:], op0=MULT, op1=ADD)
 
         def store(n0, n1):
             g, t0 = divmod(n0, TILES)
             nc.sync.dma_start(
                 out=o_v[g][:, t0 : t0 + n1 - n0, :],
-                in_=o_of[n0 // QUAD][:, n0 % QUAD : n0 % QUAD + n1 - n0, :],
+                in_=o_of[g][:, t0 : t0 + n1 - n0, :],
             )
 
         transpose_x(0)
@@ -239,5 +237,7 @@ def tile_lorasequential_pa_t_kernel(tc, x, h_lora, lora_B, M, out):
                 store(b, b + 1)
             elif i >= PAIRS - 4:
                 store(a, b + 1)
-            elif i % 2 == 1:
+            elif g == SEGS - 2 and s % 2 == 1:
                 store(a - 2, b + 1)
+            elif g < SEGS - 2 and s == 3:
+                store(a - 6, b + 1)

@@ -66,11 +66,13 @@ def tile_lorasequential_pa_t_kernel(tc, x, h_lora, lora_B, M, out):
         def load_b(g0, g1):
             nc.sync.dma_start(out=b_sb[:, g0:g1, :], in_=b_v[:, g0:g1, :])
 
+        nc.sync.dma_start(out=h_sb[:, 0, 0 : HALF * RANK], in_=h_v[:, 0, 0 : HALF * RANK])
         load_x(0, 0, 2)
-        load_h(0, 1)
+        nc.sync.dma_start(out=h_sb[:, 0, HALF * RANK :], in_=h_v[:, 0, HALF * RANK :])
         load_b(0, 1)
         nc.sync.dma_start(out=m_raw[:].rearrange("p (u e) c -> p u (e c)", u=2), in_=m_v)
-        load_x(0, 2, 8)
+        load_x(0, 2, 4)
+        load_x(0, 4, 8)
         load_h(1, 2)
         load_b(1, 2)
         load_x(1, 0, 8)
@@ -179,22 +181,22 @@ def tile_lorasequential_pa_t_kernel(tc, x, h_lora, lora_B, M, out):
                 in_=o_of[g][:, t0 : t0 + n1 - n0, :],
             )
 
-        transpose_x(0)
-        copy_x(0)
         hp = ps_h.tile([P, TILES, P], BF16)
         transpose_h(0, hp, 0, HALF)
         copy_h(0, hp, 0, HALF)
+        transpose_x(0)
+        copy_x(0)
+        transpose_h(0, hp, HALF, TILES)
+        copy_h(0, hp, HALF, TILES)
         quantise_x(0)
+        lo_of = {0: lora(0), 1: lora(1)}
+        lora_out(0, lo_of[0])
         interleave_m(nc.scalar.copy, 0, M_SHARE)
         interleave_m(nc.vector.tensor_copy, M_SHARE, OUT_F)
         quantise_m()
-        lo_of = {0: lora(0), 1: lora(1)}
-        lora_out(0, lo_of[0])
         lora_out(1, lo_of[1])
         transpose_x(1)
         copy_x(1)
-        transpose_h(0, hp, HALF, TILES)
-        copy_h(0, hp, HALF, TILES)
 
         for i in range(PAIRS):
             a, b = 2 * i, 2 * i + 1
@@ -202,10 +204,6 @@ def tile_lorasequential_pa_t_kernel(tc, x, h_lora, lora_B, M, out):
             s = i % 4
             more_h = g + 1 < SEGS
             more_l = i + 1 < PAIRS
-            early = i == 0
-            if early:
-                mx_a = base(a)
-                mx_b = base(b)
             if more_l:
                 lo_of[a + 2] = lora(a + 2)
             if i + 2 < PAIRS:
@@ -217,9 +215,8 @@ def tile_lorasequential_pa_t_kernel(tc, x, h_lora, lora_B, M, out):
                 transpose_h(g + 1, hp, TILES // 2, TILES)
             if more_l:
                 lo_of[b + 2] = lora(b + 2)
-            if not early:
-                mx_a = base(a)
-                mx_b = base(b)
+            mx_a = base(a)
+            mx_b = base(b)
             if more_l:
                 lora_out(a + 2, lo_of[a + 2])
                 lora_out(b + 2, lo_of[b + 2])
@@ -227,12 +224,12 @@ def tile_lorasequential_pa_t_kernel(tc, x, h_lora, lora_B, M, out):
                 copy_x(i + 2)
             if i + 1 < PAIRS:
                 quantise_x(i + 1)
+            if more_h and s == 1:
+                copy_h(g + 1, hp, 0, TILES)
             add_base(a, mx_a)
             if i == PAIRS - 1:
                 store(a, a + 1)
             add_base(b, mx_b)
-            if more_h and s == 1:
-                copy_h(g + 1, hp, 0, TILES)
             if i == PAIRS - 1:
                 store(b, b + 1)
             elif i >= PAIRS - 4:

@@ -66,26 +66,18 @@ def tile_lorasequential_pa_t_kernel(tc, x, h_lora, lora_B, M, out):
         def load_b(g0, g1):
             nc.sync.dma_start(out=b_sb[:, g0:g1, :], in_=b_v[:, g0:g1, :])
 
-        nc.sync.dma_start(out=h_sb[:, 0, 0 : HALF * RANK], in_=h_v[:, 0, 0 : HALF * RANK])
         load_x(0, 0, 2)
-        nc.sync.dma_start(out=h_sb[:, 0, HALF * RANK :], in_=h_v[:, 0, HALF * RANK :])
+        load_h(0, 1)
         load_b(0, 1)
         nc.sync.dma_start(out=m_raw[:].rearrange("p (u e) c -> p u (e c)", u=2), in_=m_v)
-        load_x(0, 2, 4)
-        load_x(0, 4, 8)
+        load_x(0, 2, 8)
         load_h(1, 2)
         load_b(1, 2)
         load_x(1, 0, 8)
-        load_x(2, 0, 8)
-        load_h(2, 4)
-        load_b(2, 4)
-        load_x(3, 0, 8)
-        load_x(4, 0, 8)
-        load_h(4, 8)
-        load_b(4, 8)
-        load_x(5, 0, 8)
-        load_x(6, 0, 8)
-        load_x(7, 0, 8)
+        load_h(2, 8)
+        load_b(2, 8)
+        for g in range(2, SEGS):
+            load_x(g, 0, 8)
 
         m_grp = keep.tile([P, OUT_F, 4], BF16, align_bytes=64)
         m_codes = keep.tile([P, OUT_F], U32, align_bytes=64)
@@ -181,20 +173,20 @@ def tile_lorasequential_pa_t_kernel(tc, x, h_lora, lora_B, M, out):
                 in_=o_of[g][:, t0 : t0 + n1 - n0, :],
             )
 
+        transpose_x(0)
+        copy_x(0)
         hp = ps_h.tile([P, TILES, P], BF16)
         transpose_h(0, hp, 0, HALF)
         copy_h(0, hp, 0, HALF)
-        transpose_x(0)
-        copy_x(0)
-        transpose_h(0, hp, HALF, TILES)
-        copy_h(0, hp, HALF, TILES)
         quantise_x(0)
         lo_of = {0: lora(0), 1: lora(1)}
-        lora_out(0, lo_of[0])
         interleave_m(nc.scalar.copy, 0, M_SHARE)
         interleave_m(nc.vector.tensor_copy, M_SHARE, OUT_F)
         quantise_m()
+        lora_out(0, lo_of[0])
         lora_out(1, lo_of[1])
+        transpose_h(0, hp, HALF, TILES)
+        copy_h(0, hp, HALF, TILES)
         transpose_x(1)
         copy_x(1)
 
@@ -224,12 +216,12 @@ def tile_lorasequential_pa_t_kernel(tc, x, h_lora, lora_B, M, out):
                 copy_x(i + 2)
             if i + 1 < PAIRS:
                 quantise_x(i + 1)
-            if more_h and s == 1:
-                copy_h(g + 1, hp, 0, TILES)
             add_base(a, mx_a)
             if i == PAIRS - 1:
                 store(a, a + 1)
             add_base(b, mx_b)
+            if more_h and s == 1:
+                copy_h(g + 1, hp, 0, TILES)
             if i == PAIRS - 1:
                 store(b, b + 1)
             elif i >= PAIRS - 4:

@@ -74,10 +74,16 @@ def tile_lorasequential_pa_t_kernel(tc, x, h_lora, lora_B, M, out):
         load_h(1, 2)
         load_b(1, 2)
         load_x(1, 0, 8)
-        load_h(2, 8)
-        load_b(2, 8)
-        for g in range(2, SEGS):
-            load_x(g, 0, 8)
+        load_x(2, 0, 8)
+        load_h(2, 4)
+        load_b(2, 4)
+        load_x(3, 0, 8)
+        load_x(4, 0, 8)
+        load_h(4, 8)
+        load_b(4, 8)
+        load_x(5, 0, 8)
+        load_x(6, 0, 8)
+        load_x(7, 0, 8)
 
         m_grp = keep.tile([P, OUT_F, 4], BF16, align_bytes=64)
         m_codes = keep.tile([P, OUT_F], U32, align_bytes=64)

from contextlib import ExitStack

import concourse.mybir as mybir
from concourse.masks import make_identity

F32 = mybir.dt.float32
BF16 = mybir.dt.bfloat16
U32 = mybir.dt.uint32
U8 = mybir.dt.uint8
FP8X4 = mybir.dt.float8_e4m3fn_x4
ADD = mybir.AluOpType.add
MULT = mybir.AluOpType.mult

P = 128
ROWS, IN_F, OUT_F, RANK, SEGS = 8192, 512, 512, 128, 8
SEG_ROWS = ROWS // SEGS
TILES = SEG_ROWS // P
WORDS = IN_F // 2
PAIRS = SEGS * TILES // 2
HALF = TILES // 2
M_SHARE = 128
GAIN = 2.0

FLOPS = 2 * ROWS * IN_F * OUT_F + 2 * ROWS * RANK * OUT_F

STAGE_BUFS = 6
LO_BANKS = 2
MX_BANKS = 3


def tile_lorasequential_pa_t_kernel(tc, x, h_lora, lora_B, M, out):
    nc = tc.nc
    with ExitStack() as ctx:
        ctx.enter_context(tc.manual_schedule())
        keep = ctx.enter_context(tc.tile_pool(name="keep", bufs=1))
        grp_pool = ctx.enter_context(tc.tile_pool(name="grp", bufs=3))
        ht_pool = ctx.enter_context(tc.tile_pool(name="ht", bufs=2))
        stage = ctx.enter_context(tc.tile_pool(name="stage", bufs=STAGE_BUFS))
        ps_x = ctx.enter_context(tc.psum_pool(name="psx", bufs=2))
        ps_h = ctx.enter_context(tc.psum_pool(name="psh", bufs=1))
        ps_l = ctx.enter_context(tc.psum_pool(name="psl", bufs=LO_BANKS))
        ps_m = ctx.enter_context(tc.psum_pool(name="psm", bufs=MX_BANKS))

        x_v = x.rearrange("(g p t) k -> g p (t k)", p=P, t=TILES)
        h_v = h_lora.rearrange("g (p t) r -> p g (t r)", t=TILES)
        b_v = lora_B.rearrange("g r n -> r g n")
        m_v = M.rearrange("(u q e) c -> q u (e c)", u=2, e=2)
        o_v = out.rearrange("(g p t) n -> g p t n", p=P, t=TILES)

        ident_f = keep.tile([P, P], F32)
        make_identity(nc, ident_f[:])
        ident_b = keep.tile([P, P], BF16)
        make_identity(nc, ident_b[:])

        m_raw = keep.tile([P, 4, OUT_F], BF16)
        x_sb = [keep.tile([P, TILES * IN_F], BF16, name="x%d" % g) for g in range(SEGS)]
        h_sb = keep.tile([P, SEGS, TILES * RANK], BF16)
        b_sb = keep.tile([P, SEGS, OUT_F], BF16)

        def load_x(g, t0, t1):
            nc.sync.dma_start(out=x_sb[g][:, t0 * IN_F : t1 * IN_F], in_=x_v[g][:, t0 * IN_F : t1 * IN_F])

        def load_h(g0, g1):
            nc.sync.dma_start(out=h_sb[:, g0:g1, :], in_=h_v[:, g0:g1, :])

        def load_b(g0, g1):
            nc.sync.dma_start(out=b_sb[:, g0:g1, :], in_=b_v[:, g0:g1, :])

        load_x(0, 0, 2)
        load_h(0, 1)
        load_b(0, 1)
        nc.sync.dma_start(out=m_raw[:].rearrange("p (u e) c -> p u (e c)", u=2), in_=m_v)
        load_x(0, 2, 8)
        load_h(1, 2)
        load_b(1, 2)
        load_x(1, 0, 8)
        load_x(2, 0, 8)
        load_h(2, 4)
        load_b(2, 4)
        load_x(3, 0, 8)
        load_x(4, 0, 8)
        load_h(4, 8)
        load_b(4, 8)
        load_x(5, 0, 8)
        load_x(6, 0, 8)
        load_x(7, 0, 8)

        m_grp = keep.tile([P, OUT_F, 4], BF16, align_bytes=64)
        m_codes = keep.tile([P, OUT_F], U32, align_bytes=64)
        m_scales = keep.tile([P, OUT_F], U8, align_bytes=64)

        def interleave_m(copy, c0, c1):
            copy(out=m_grp[:, c0:c1, :], in_=m_raw[:, :, c0:c1].rearrange("p t c -> p c t"))

        def quantise_m():
            nc.vector.quantize_mx(
                out=m_codes[:].bitcast(FP8X4),
                scales=m_scales[:],
                in_=m_grp[:].rearrange("p c t -> p (c t)"),
            )

        xt_of = {}
        grp_of = {}
        q_of = {}
        ht_of = {}
        o_of = {}

        def transpose_x(i):
            xt = ps_x.tile([P, 2, 2 * P], F32)
            for j in range(2):
                g, t = divmod(2 * i + j, TILES)
                words = x_sb[g][:].bitcast(F32)
                for u in range(2):
                    w0 = t * WORDS + u * P
                    nc.tensor.transpose(xt[:, u, j * P : (j + 1) * P], words[:, w0 : w0 + P], ident_f[:])
            xt_of[i] = xt

        def copy_x(i):
            grp = grp_pool.tile([P, 8 * P], BF16, align_bytes=64)
            nc.scalar.copy(
                out=grp[:].bitcast(F32).rearrange("p (c u) -> p c u", u=2),
                in_=xt_of[i][:].rearrange("p u c -> p c u"),
            )
            grp_of[i] = grp

        def quantise_x(i):
            codes = grp_pool.tile([P, 2 * P], U32, align_bytes=64)
            scales = grp_pool.tile([P, 2 * P], U8, align_bytes=64)
            nc.vector.quantize_mx(out=codes[:].bitcast(FP8X4), scales=scales[:], in_=grp_of[i][:])
            q_of[i] = (codes, scales)

        def transpose_h(g, hp, t0, t1):
            for t in range(t0, t1):
                nc.tensor.transpose(hp[:, t, :], h_sb[:, g, t * RANK : (t + 1) * RANK], ident_b[:])

        def copy_h(g, hp, t0, t1):
            if t0 == 0:
                ht = ht_pool.tile([P, TILES, P], BF16)
                ht_of[g] = ht
            nc.vector.tensor_copy(out=ht_of[g][:, t0:t1, :], in_=hp[:, t0:t1, :])

        def lora(n):
            g, t = divmod(n, TILES)
            lo = ps_l.tile([P, OUT_F], F32)
            nc.tensor.matmul(lo[:], lhsT=ht_of[g][:, t, :], rhs=b_sb[:, g, :], start=True, stop=True)
            return lo

        def base(n):
            codes, scales = q_of[n // 2]
            cols = slice((n % 2) * P, (n % 2 + 1) * P)
            mx = ps_m.tile([P, OUT_F], F32)
            nc.tensor.matmul_mx(
                out=mx[:],
                lhsT=codes[:, cols].bitcast(FP8X4),
                lhsT_scale=scales[:, cols],
                rhs=m_codes[:].bitcast(FP8X4),
                rhs_scale=m_scales[:],
                start=True,
                stop=True,
            )
            return mx

        def lora_out(n, lo):
            g, t = divmod(n, TILES)
            if t == 0:
                o_sb = stage.tile([P, TILES, OUT_F], F32)
                o_of[g] = o_sb
            nc.scalar.copy(out=o_of[g][:, t, :], in_=lo[:])

        def add_base(n, mx):
            g, t = divmod(n, TILES)
            o_part = o_of[g][:, t, :]
            nc.vector.scalar_tensor_tensor(out=o_part, in0=o_part, scalar=GAIN, in1=mx[:], op0=MULT, op1=ADD)

        def store(n0, n1):
            g, t0 = divmod(n0, TILES)
            nc.sync.dma_start(
                out=o_v[g][:, t0 : t0 + n1 - n0, :],
                in_=o_of[g][:, t0 : t0 + n1 - n0, :],
            )

        transpose_x(0)
        copy_x(0)
        hp = ps_h.tile([P, TILES, P], BF16)
        transpose_h(0, hp, 0, HALF)
        copy_h(0, hp, 0, HALF)
        quantise_x(0)
        lo_of = {0: lora(0), 1: lora(1)}
        interleave_m(nc.scalar.copy, 0, M_SHARE)
        interleave_m(nc.vector.tensor_copy, M_SHARE, OUT_F)
        quantise_m()
        lora_out(0, lo_of[0])
        lora_out(1, lo_of[1])
        transpose_h(0, hp, HALF, TILES)
        copy_h(0, hp, HALF, TILES)
        transpose_x(1)
        copy_x(1)

        for i in range(PAIRS):
            a, b = 2 * i, 2 * i + 1
            g = a // TILES
            s = i % 4
            more_h = g + 1 < SEGS
            more_l = i + 1 < PAIRS
            if more_l:
                lo_of[a + 2] = lora(a + 2)
            if i + 2 < PAIRS:
                transpose_x(i + 2)
            if more_h and s == 0:
                hp = ps_h.tile([P, TILES, P], BF16)
                transpose_h(g + 1, hp, 0, TILES // 2)
            if more_h and s == 1:
                transpose_h(g + 1, hp, TILES // 2, TILES)
            if more_l:
                lo_of[b + 2] = lora(b + 2)
            mx_a = base(a)
            mx_b = base(b)
            if more_l:
                lora_out(a + 2, lo_of[a + 2])
                lora_out(b + 2, lo_of[b + 2])
            if i + 2 < PAIRS:
                copy_x(i + 2)
            if i + 1 < PAIRS:
                quantise_x(i + 1)
            add_base(a, mx_a)
            if i == PAIRS - 1:
                store(a, a + 1)
            add_base(b, mx_b)
            if more_h and s == 1:
                copy_h(g + 1, hp, 0, TILES)
            if i == PAIRS - 1:
                store(b, b + 1)
            elif i >= PAIRS - 4:
                store(a, b + 1)
            elif g == SEGS - 2 and s % 2 == 1:
                store(a - 2, b + 1)
            elif g < SEGS - 2 and s == 3:
                store(a - 6, b + 1)
